import numpy as np
import ml_dtypes


def mxq(x, axis, fmt="e4m3"):
    dtype, down = {"e4m3": (ml_dtypes.float8_e4m3fn, 7), "e5m2": (ml_dtypes.float8_e5m2, 14)}[fmt]
    v = np.moveaxis(np.asarray(x, np.float32).astype(ml_dtypes.bfloat16).astype(np.float64), axis, -1)
    blocks = v.reshape(v.shape[:-1] + (-1, 32))
    amax = np.abs(blocks).max(-1, keepdims=True)
    byte = np.maximum(np.where(amax > 0, np.frexp(amax)[1] - 1 + 127, 0) - down, 1)
    scale = np.exp2(byte - 127.0)
    codes = (blocks / scale).astype(np.float32).astype(dtype).astype(np.float64)
    return np.moveaxis((codes * scale).reshape(v.shape), -1, axis)


WIDE = False


def mx_kscale(k):
    if not WIDE:
        return np.ones(k)
    levels = np.array([20, -20, 10, -10, 0])
    a = np.random.permutation(np.resize(levels, k // 512 * 4)).reshape(k // 512, 4)
    idx = np.arange(k)
    return np.exp2(a[idx // 512, idx % 128 // 32])


BF16 = ml_dtypes.bfloat16


def bf(x):
    return np.asarray(x, np.float32).astype(BF16)


def f64(x):
    return np.asarray(x).astype(np.float64)


B, S, K, N = 4, 256, 4096, 1024

GRID_VALUES = np.array([-6.0, -4.0, -3.0, -2.0, -1.5, -1.0, -0.5, 0.0, 0.5, 1.0, 1.5, 2.0, 3.0, 4.0, 6.0], dtype=np.float32)


def setup_inputs():
    u = mx_kscale(N)
    x = np.random.standard_normal((B, S, K))
    weight = np.random.standard_normal((N, K)) * 0.02 / u[:, None]
    bias = np.random.standard_normal(N) * 0.3
    g = np.random.standard_normal((B, S, N)) * np.exp2(np.random.randint(-12, 1, (B, S, 1))) * 8.0 * u
    return {"x": bf(x), "weight": bf(weight), "bias": bf(bias), "grid": bf(GRID_VALUES), "grad_out": bf(g)}


def reference(x, weight, bias, grid, grad_out):
    g2d = f64(grad_out).reshape(-1, weight.shape[0])
    gx = mxq(g2d, 1, "e5m2") @ mxq(f64(weight), 0, "e4m3")
    return gx.reshape(x.shape)

@@ -1,0 +1,171 @@
+from contextlib import ExitStack
+
+import concourse.mybir as mybir
+from concourse.masks import make_identity
+
+F32 = mybir.dt.float32
+BF16 = mybir.dt.bfloat16
+U32 = mybir.dt.uint32
+U8 = mybir.dt.uint8
+E4X4 = mybir.dt.float8_e4m3fn_x4
+E5X4 = mybir.dt.float8_e5m2_x4
+
+P = 128
+TOKENS = 1024
+K = 1024
+COLS = 4096
+T_TILES = TOKENS // P
+PASSES = K // 512
+NB = 512
+BLOCKS = COLS // NB
+
+FLOPS = 2 * TOKENS * K * COLS
+BYTES = K * COLS * 2 + TOKENS * K * 2 + TOKENS * COLS * 4
+
+MANUAL = False
+LOAD_GROUPS = ((0, 1024), (1024, 1024), (2048, 2048))
+SCALAR_REGROUPS = ((1, 0), (1, 1))
+VECTOR_EVAC_FROM_BLOCK = 5
+STAGE_BUFS = 16
+GRP_BUFS = 5
+
+
+def tile_ant_linear_kernel(tc, x, weight, bias, grid, grad_out, out):
+    nc = tc.nc
+    g_view = grad_out.flatten_outer_dims().rearrange("(p t) k -> p (t k)", t=T_TILES)
+    o_view = out.flatten_outer_dims().rearrange("(p t) i -> p t i", t=T_TILES)
+    w_view = weight.rearrange("(c u q e) i -> c u q e i", c=PASSES, u=2, e=2)
+
+    with ExitStack() as ctx:
+        keep = ctx.enter_context(tc.tile_pool(name="keep", bufs=1))
+        ring = ctx.enter_context(tc.tile_pool(name="ring", bufs=GRP_BUFS))
+        stages = ctx.enter_context(tc.tile_pool(name="stages", bufs=STAGE_BUFS))
+        psum = ctx.enter_context(tc.psum_pool(name="psum", bufs=8))
+        if MANUAL:
+            ctx.enter_context(tc.manual_schedule())
+
+        g_raw = []
+        for hb in range(2):
+            t_raw = ring.tile([P, 4096], BF16, tag="ring", name="graw%d" % hb, align_bytes=64)
+            nc.sync.dma_start(out=t_raw[:], in_=g_view[:, 4096 * hb : 4096 * (hb + 1)])
+            g_raw.append(t_raw)
+        w_raw = []
+        for gi, (c0, width) in enumerate(LOAD_GROUPS):
+            per_pass = []
+            for c in range(PASSES):
+                t_w = keep.tile([P, 4, width], BF16, name="wraw%d_%d" % (gi, c))
+                for u in range(2):
+                    nc.sync.dma_start(
+                        out=t_w[:, 2 * u : 2 * u + 2, :],
+                        in_=w_view[c, u, :, :, c0 : c0 + width],
+                    )
+                per_pass.append(t_w)
+            w_raw.append(per_pass)
+
+        ident = keep.tile([P, P], F32, name="ident")
+        make_identity(nc, ident[:])
+
+        g_codes = []
+        g_scales = []
+        for hb in range(2):
+            words = g_raw[hb][:].bitcast(F32)
+            g_grp = ring.tile([P, 2048], F32, tag="ring", name="ggrp%d" % hb, align_bytes=64)
+            for tl in range(4):
+                xt = psum.tile([P, 512], F32, tag="bank", name="xt")
+                for j in range(4):
+                    nc.tensor.transpose(
+                        xt[:, P * j : P * (j + 1)],
+                        words[:, 512 * tl + P * j : 512 * tl + P * (j + 1)],
+                        ident[:],
+                    )
+                dst = g_grp[:, 512 * tl : 512 * (tl + 1)].rearrange(
+                    "p (c r u) -> p c r u", c=2, u=2
+                )
+                src = xt[:].rearrange("p (c u r) -> p c r u", c=2, u=2)
+                if tl % 2 == 0:
+                    nc.scalar.copy(out=dst, in_=src)
+                else:
+                    nc.vector.tensor_copy(out=dst, in_=src)
+            codes = keep.tile([P, 1024], U32, name="gcodes%d" % hb, align_bytes=64)
+            scales = keep.tile([P, 1024], U8, name="gscales%d" % hb, align_bytes=64)
+            nc.vector.quantize_mx(
+                out=codes[:].bitcast(E5X4), scales=scales[:], in_=g_grp[:].bitcast(BF16)
+            )
+            g_codes.append(codes)
+            g_scales.append(scales)
+
+        w_grp = {}
+        w_codes = {}
+        w_scales = {}
+
+        def alloc(n):
+            w_grp[n] = ring.tile([P, 4096], BF16, tag="ring", name="wgrp%d" % n, align_bytes=64)
+            w_codes[n] = keep.tile([P, 1024], U32, name="wcodes%d" % n, align_bytes=64)
+            w_scales[n] = keep.tile([P, 1024], U8, name="wscales%d" % n, align_bytes=64)
+
+        def regroup(n, c):
+            col = n * NB
+            gi = [i for i, (c0, width) in enumerate(LOAD_GROUPS) if c0 <= col < c0 + width][0]
+            off = col - LOAD_GROUPS[gi][0]
+            src = w_raw[gi][c][:, :, off : off + NB].rearrange("p t (a i) -> p a t i", i=4)
+            dst = w_grp[n][:, 2048 * c : 2048 * (c + 1)].rearrange(
+                "p (a i t) -> p a t i", i=4, t=4
+            )
+            if (n, c) in SCALAR_REGROUPS:
+                nc.scalar.copy(out=dst, in_=src)
+            else:
+                nc.vector.tensor_copy(out=dst, in_=src)
+
+        def quantise(n, lo, hi):
+            nc.vector.quantize_mx(
+                out=w_codes[n][:, 512 * lo : 512 * hi].bitcast(E4X4),
+                scales=w_scales[n][:, 512 * lo : 512 * hi],
+                in_=w_grp[n][:, 2048 * lo : 2048 * hi],
+            )
+
+        alloc(0)
+        alloc(1)
+        regroup(0, 0)
+        regroup(0, 1)
+        regroup(1, 0)
+        regroup(1, 1)
+        quantise(0, 0, 1)
+        quantise(0, 1, 2)
+        quantise(1, 0, 2)
+        for n in range(2, BLOCKS):
+            alloc(n)
+            regroup(n, 0)
+            regroup(n, 1)
+            if n > 2:
+                quantise(n - 1, 0, 2)
+        quantise(BLOCKS - 1, 0, 2)
+
+        for pair in range(BLOCKS // 2):
+            stage = []
+            for t in range(T_TILES):
+                stage.append(stages.tile([P, 2 * NB], F32, tag="stage", name="stage"))
+            for half in range(2):
+                n = 2 * pair + half
+                for t in range(T_TILES):
+                    acc = psum.tile([P, NB], F32, tag="bank", name="acc")
+                    for c in range(PASSES):
+                        sl = slice(P * (2 * (t % 4) + c), P * (2 * (t % 4) + c + 1))
+                        nc.tensor.matmul_mx(
+                            out=acc[:],
+                            lhsT=g_codes[t // 4][:, sl].bitcast(E5X4),
+                            lhsT_scale=g_scales[t // 4][:, sl],
+                            rhs=w_codes[n][:, 512 * c : 512 * (c + 1)].bitcast(E4X4),
+                            rhs_scale=w_scales[n][:, 512 * c : 512 * (c + 1)],
+                            start=(c == 0),
+                            stop=(c == PASSES - 1),
+                        )
+                    dst = stage[t][:, NB * half : NB * (half + 1)]
+                    if n >= VECTOR_EVAC_FROM_BLOCK and t % 2 == 1:
+                        nc.vector.tensor_copy(out=dst, in_=acc[:])
+                    else:
+                        nc.scalar.copy(out=dst, in_=acc[:])
+                    if half == 1:
+                        nc.sync.dma_start(
+                            out=o_view[:, t, 2 * NB * pair : 2 * NB * (pair + 1)],
+                            in_=stage[t][:],
+                        )

@@ -22,7 +22,7 @@ BLOCKS = COLS // NB
 FLOPS = 2 * TOKENS * K * COLS
 BYTES = K * COLS * 2 + TOKENS * K * 2 + TOKENS * COLS * 4
 
-MANUAL = False
+MANUAL = True
 LOAD_GROUPS = ((0, 1024), (1024, 1024), (2048, 2048))
 SCALAR_REGROUPS = ((1, 0), (1, 1))
 VECTOR_EVAC_FROM_BLOCK = 5

@@ -18,16 +18,17 @@ T_TILES = TOKENS // P
 PASSES = K // 512
 NB = 512
 BLOCKS = COLS // NB
+HALF = COLS // 2
 
 FLOPS = 2 * TOKENS * K * COLS
 BYTES = K * COLS * 2 + TOKENS * K * 2 + TOKENS * COLS * 4
 
 MANUAL = True
-LOAD_GROUPS = ((0, 1024), (1024, 1024), (2048, 2048))
-SCALAR_REGROUPS = ((1, 0), (1, 1))
-VECTOR_EVAC_FROM_BLOCK = 5
-STAGE_BUFS = 16
-GRP_BUFS = 5
+STORE_GROUPS = ((0, 1, 2, 3), (4, 5, 6, 7))
+SCALAR_REGROUPS = ((2, 0), (3, 0), (1, 1), (3, 1))
+VECTOR_EVAC_FROM_BANK = 24
+TAIL_PIECES = (2, 1, 1)
+RING_BUFS = 5
 
 
 def tile_ant_linear_kernel(tc, x, weight, bias, grid, grad_out, out):
@@ -38,8 +39,8 @@ def tile_ant_linear_kernel(tc, x, weight, bias, grid, grad_out, out):
 
     with ExitStack() as ctx:
         keep = ctx.enter_context(tc.tile_pool(name="keep", bufs=1))
-        ring = ctx.enter_context(tc.tile_pool(name="ring", bufs=GRP_BUFS))
-        stages = ctx.enter_context(tc.tile_pool(name="stages", bufs=STAGE_BUFS))
+        flat = ctx.enter_context(tc.tile_pool(name="flat", bufs=1))
+        ring = ctx.enter_context(tc.tile_pool(name="ring", bufs=RING_BUFS))
         psum = ctx.enter_context(tc.psum_pool(name="psum", bufs=8))
         if MANUAL:
             ctx.enter_context(tc.manual_schedule())
@@ -50,14 +51,16 @@ def tile_ant_linear_kernel(tc, x, weight, bias, grid, grad_out, out):
             nc.sync.dma_start(out=t_raw[:], in_=g_view[:, 4096 * hb : 4096 * (hb + 1)])
             g_raw.append(t_raw)
         w_raw = []
-        for gi, (c0, width) in enumerate(LOAD_GROUPS):
+        for h in range(2):
             per_pass = []
             for c in range(PASSES):
-                t_w = keep.tile([P, 4, width], BF16, name="wraw%d_%d" % (gi, c))
+                t_w = flat.tile(
+                    [P, 4, HALF], BF16, name="wraw%d_%d" % (h, c), offset=16384 * (2 * h + c)
+                )
                 for u in range(2):
                     nc.sync.dma_start(
                         out=t_w[:, 2 * u : 2 * u + 2, :],
-                        in_=w_view[c, u, :, :, c0 : c0 + width],
+                        in_=w_view[c, u, :, :, HALF * h : HALF * (h + 1)],
                     )
                 per_pass.append(t_w)
             w_raw.append(per_pass)
@@ -104,10 +107,8 @@ def tile_ant_linear_kernel(tc, x, weight, bias, grid, grad_out, out):
             w_scales[n] = keep.tile([P, 1024], U8, name="wscales%d" % n, align_bytes=64)
 
         def regroup(n, c):
-            col = n * NB
-            gi = [i for i, (c0, width) in enumerate(LOAD_GROUPS) if c0 <= col < c0 + width][0]
-            off = col - LOAD_GROUPS[gi][0]
-            src = w_raw[gi][c][:, :, off : off + NB].rearrange("p t (a i) -> p a t i", i=4)
+            off = (n % 4) * NB
+            src = w_raw[n // 4][c][:, :, off : off + NB].rearrange("p t (a i) -> p a t i", i=4)
             dst = w_grp[n][:, 2048 * c : 2048 * (c + 1)].rearrange(
                 "p (a i t) -> p a t i", i=4, t=4
             )
@@ -123,30 +124,41 @@ def tile_ant_linear_kernel(tc, x, weight, bias, grid, grad_out, out):
                 in_=w_grp[n][:, 2048 * lo : 2048 * hi],
             )
 
-        alloc(0)
-        alloc(1)
-        regroup(0, 0)
-        regroup(0, 1)
-        regroup(1, 0)
-        regroup(1, 1)
-        quantise(0, 0, 1)
-        quantise(0, 1, 2)
-        quantise(1, 0, 2)
-        for n in range(2, BLOCKS):
+        for n in range(4):
             alloc(n)
+        for n in range(4):
             regroup(n, 0)
+        for n in range(4):
+            quantise(n, 0, 1)
+        for n in (0, 2, 1, 3):
             regroup(n, 1)
-            if n > 2:
-                quantise(n - 1, 0, 2)
-        quantise(BLOCKS - 1, 0, 2)
+        for n in range(4):
+            quantise(n, 1, 2)
+        for n in range(4, 8):
+            alloc(n)
+        for n in range(4, 8):
+            regroup(n, 0)
+        regroup(4, 1)
+        regroup(5, 1)
+        quantise(4, 0, 2)
+        regroup(6, 1)
+        quantise(5, 0, 2)
+        regroup(7, 1)
+        quantise(6, 0, 2)
+        quantise(7, 0, 2)
 
-        for pair in range(BLOCKS // 2):
-            stage = []
+        bank = 0
+        for gi, blocks in enumerate(STORE_GROUPS):
+            col0 = blocks[0] * NB
+            width = len(blocks) * NB
             for t in range(T_TILES):
-                stage.append(stages.tile([P, 2 * NB], F32, tag="stage", name="stage"))
-            for half in range(2):
-                n = 2 * pair + half
-                for t in range(T_TILES):
+                base = (0 if col0 >= HALF else 65536) + 8192 * t + 4 * (col0 % HALF)
+                stage = flat.tile([P, width], F32, name="stage%d_%d" % (gi, t), offset=base)
+                last = gi == len(STORE_GROUPS) - 1 and t == T_TILES - 1
+                pieces = TAIL_PIECES if last else (len(blocks),)
+                done = 0
+                stored = 0
+                for n in blocks:
                     acc = psum.tile([P, NB], F32, tag="bank", name="acc")
                     for c in range(PASSES):
                         sl = slice(P * (2 * (t % 4) + c), P * (2 * (t % 4) + c + 1))
@@ -159,13 +171,17 @@ def tile_ant_linear_kernel(tc, x, weight, bias, grid, grad_out, out):
                             start=(c == 0),
                             stop=(c == PASSES - 1),
                         )
-                    dst = stage[t][:, NB * half : NB * (half + 1)]
-                    if n >= VECTOR_EVAC_FROM_BLOCK and t % 2 == 1:
+                    dst = stage[:, NB * done : NB * (done + 1)]
+                    if bank >= VECTOR_EVAC_FROM_BANK and bank % 2 == 1:
                         nc.vector.tensor_copy(out=dst, in_=acc[:])
                     else:
                         nc.scalar.copy(out=dst, in_=acc[:])
-                    if half == 1:
+                    bank += 1
+                    done += 1
+                    if done - stored == pieces[0]:
                         nc.sync.dma_start(
-                            out=o_view[:, t, 2 * NB * pair : 2 * NB * (pair + 1)],
-                            in_=stage[t][:],
+                            out=o_view[:, t, col0 + NB * stored : col0 + NB * done],
+                            in_=stage[:, NB * stored : NB * done],
                         )
+                        stored = done
+                        pieces = pieces[1:]

@@ -24,10 +24,10 @@ FLOPS = 2 * TOKENS * K * COLS
 BYTES = K * COLS * 2 + TOKENS * K * 2 + TOKENS * COLS * 4
 
 MANUAL = True
-STORE_GROUPS = ((0, 1, 2, 3), (4, 5, 6, 7))
-SCALAR_REGROUPS = ((2, 0), (3, 0), (1, 1), (3, 1))
-VECTOR_EVAC_FROM_BANK = 24
-TAIL_PIECES = (2, 1, 1)
+LOAD_GROUPS = ((0, 1024), (1024, 1024), (2048, 2048))
+SCALAR_REGROUPS = ((1, 0), (1, 1), (3, 0), (3, 1))
+VECTOR_EVAC_FROM_BANK = 32
+TAIL_STORES_AFTER = (5, 6, 7)
 RING_BUFS = 5
 
 
@@ -51,16 +51,19 @@ def tile_ant_linear_kernel(tc, x, weight, bias, grid, grad_out, out):
             nc.sync.dma_start(out=t_raw[:], in_=g_view[:, 4096 * hb : 4096 * (hb + 1)])
             g_raw.append(t_raw)
         w_raw = []
-        for h in range(2):
+        for c0, width in LOAD_GROUPS:
             per_pass = []
             for c in range(PASSES):
                 t_w = flat.tile(
-                    [P, 4, HALF], BF16, name="wraw%d_%d" % (h, c), offset=16384 * (2 * h + c)
+                    [P, 4, width],
+                    BF16,
+                    name="wraw%d_%d" % (c0, c),
+                    offset=16 * c0 + 8 * width * c,
                 )
                 for u in range(2):
                     nc.sync.dma_start(
                         out=t_w[:, 2 * u : 2 * u + 2, :],
-                        in_=w_view[c, u, :, :, HALF * h : HALF * (h + 1)],
+                        in_=w_view[c, u, :, :, c0 : c0 + width],
                     )
                 per_pass.append(t_w)
             w_raw.append(per_pass)
@@ -107,8 +110,10 @@ def tile_ant_linear_kernel(tc, x, weight, bias, grid, grad_out, out):
             w_scales[n] = keep.tile([P, 1024], U8, name="wscales%d" % n, align_bytes=64)
 
         def regroup(n, c):
-            off = (n % 4) * NB
-            src = w_raw[n // 4][c][:, :, off : off + NB].rearrange("p t (a i) -> p a t i", i=4)
+            col = n * NB
+            gi = [i for i, (c0, width) in enumerate(LOAD_GROUPS) if c0 <= col < c0 + width][0]
+            off = col - LOAD_GROUPS[gi][0]
+            src = w_raw[gi][c][:, :, off : off + NB].rearrange("p t (a i) -> p a t i", i=4)
             dst = w_grp[n][:, 2048 * c : 2048 * (c + 1)].rearrange(
                 "p (a i t) -> p a t i", i=4, t=4
             )
@@ -126,14 +131,20 @@ def tile_ant_linear_kernel(tc, x, weight, bias, grid, grad_out, out):
 
         for n in range(4):
             alloc(n)
-        for n in range(4):
-            regroup(n, 0)
-        for n in range(4):
-            quantise(n, 0, 1)
-        for n in (0, 2, 1, 3):
-            regroup(n, 1)
-        for n in range(4):
-            quantise(n, 1, 2)
+        regroup(0, 0)
+        regroup(0, 1)
+        regroup(1, 0)
+        regroup(1, 1)
+        quantise(0, 0, 1)
+        quantise(0, 1, 2)
+        quantise(1, 0, 2)
+        regroup(2, 0)
+        regroup(2, 1)
+        regroup(3, 0)
+        regroup(3, 1)
+        quantise(2, 0, 1)
+        quantise(2, 1, 2)
+        quantise(3, 0, 2)
         for n in range(4, 8):
             alloc(n)
         for n in range(4, 8):
@@ -147,41 +158,44 @@ def tile_ant_linear_kernel(tc, x, weight, bias, grid, grad_out, out):
         quantise(6, 0, 2)
         quantise(7, 0, 2)
 
-        bank = 0
-        for gi, blocks in enumerate(STORE_GROUPS):
-            col0 = blocks[0] * NB
-            width = len(blocks) * NB
-            for t in range(T_TILES):
-                base = (0 if col0 >= HALF else 65536) + 8192 * t + 4 * (col0 % HALF)
-                stage = flat.tile([P, width], F32, name="stage%d_%d" % (gi, t), offset=base)
-                last = gi == len(STORE_GROUPS) - 1 and t == T_TILES - 1
-                pieces = TAIL_PIECES if last else (len(blocks),)
-                done = 0
-                stored = 0
-                for n in blocks:
-                    acc = psum.tile([P, NB], F32, tag="bank", name="acc")
-                    for c in range(PASSES):
-                        sl = slice(P * (2 * (t % 4) + c), P * (2 * (t % 4) + c + 1))
-                        nc.tensor.matmul_mx(
-                            out=acc[:],
-                            lhsT=g_codes[t // 4][:, sl].bitcast(E5X4),
-                            lhsT_scale=g_scales[t // 4][:, sl],
-                            rhs=w_codes[n][:, 512 * c : 512 * (c + 1)].bitcast(E4X4),
-                            rhs_scale=w_scales[n][:, 512 * c : 512 * (c + 1)],
-                            start=(c == 0),
-                            stop=(c == PASSES - 1),
-                        )
-                    dst = stage[:, NB * done : NB * (done + 1)]
-                    if bank >= VECTOR_EVAC_FROM_BANK and bank % 2 == 1:
-                        nc.vector.tensor_copy(out=dst, in_=acc[:])
-                    else:
-                        nc.scalar.copy(out=dst, in_=acc[:])
-                    bank += 1
-                    done += 1
-                    if done - stored == pieces[0]:
-                        nc.sync.dma_start(
-                            out=o_view[:, t, col0 + NB * stored : col0 + NB * done],
-                            in_=stage[:, NB * stored : NB * done],
-                        )
-                        stored = done
-                        pieces = pieces[1:]
+        order = [(0, t) for t in range(T_TILES)]
+        order += [(n, t) for t in range(T_TILES) for n in (1, 2, 3)]
+        order += [(n, t) for t in range(T_TILES) for n in (4, 5, 6, 7)]
+        stage = {}
+        stored = {}
+        filled = {}
+        for bank, (n, t) in enumerate(order):
+            h = n // 4
+            key = (h, t)
+            if key not in stage:
+                stage[key] = flat.tile(
+                    [P, HALF], F32, name="stage%d_%d" % key, offset=65536 * (1 - h) + 8192 * t
+                )
+                stored[key] = 0
+                filled[key] = 0
+            acc = psum.tile([P, NB], F32, tag="bank", name="acc")
+            for c in range(PASSES):
+                sl = slice(P * (2 * (t % 4) + c), P * (2 * (t % 4) + c + 1))
+                nc.tensor.matmul_mx(
+                    out=acc[:],
+                    lhsT=g_codes[t // 4][:, sl].bitcast(E5X4),
+                    lhsT_scale=g_scales[t // 4][:, sl],
+                    rhs=w_codes[n][:, 512 * c : 512 * (c + 1)].bitcast(E4X4),
+                    rhs_scale=w_scales[n][:, 512 * c : 512 * (c + 1)],
+                    start=(c == 0),
+                    stop=(c == PASSES - 1),
+                )
+            dst = stage[key][:, NB * (n % 4) : NB * (n % 4 + 1)]
+            if bank >= VECTOR_EVAC_FROM_BANK and bank % 2 == 1:
+                nc.vector.tensor_copy(out=dst, in_=acc[:])
+            else:
+                nc.scalar.copy(out=dst, in_=acc[:])
+            filled[key] = filled[key] + 1
+            last_tile = key == (1, T_TILES - 1)
+            if filled[key] == 4 or (last_tile and n in TAIL_STORES_AFTER):
+                lo = NB * stored[key]
+                hi = NB * filled[key]
+                nc.sync.dma_start(
+                    out=o_view[:, t, HALF * h + lo : HALF * h + hi], in_=stage[key][:, lo:hi]
+                )
+                stored[key] = filled[key]

@@ -25,7 +25,8 @@ BYTES = K * COLS * 2 + TOKENS * K * 2 + TOKENS * COLS * 4
 
 MANUAL = True
 LOAD_GROUPS = ((0, 1024), (1024, 1024), (2048, 2048))
-SCALAR_REGROUPS = ((1, 0), (1, 1), (3, 0), (3, 1))
+SCALAR_REGROUPS = ((1, 0), (1, 1))
+HEAD_SPLIT = 2
 VECTOR_EVAC_FROM_BANK = 32
 TAIL_STORES_AFTER = (5, 6, 7)
 RING_BUFS = 5
@@ -141,10 +142,10 @@ def tile_ant_linear_kernel(tc, x, weight, bias, grid, grad_out, out):
         regroup(2, 0)
         regroup(2, 1)
         regroup(3, 0)
+        quantise(2, 0, 2)
         regroup(3, 1)
-        quantise(2, 0, 1)
-        quantise(2, 1, 2)
-        quantise(3, 0, 2)
+        quantise(3, 0, 1)
+        quantise(3, 1, 2)
         for n in range(4, 8):
             alloc(n)
         for n in range(4, 8):
@@ -158,8 +159,10 @@ def tile_ant_linear_kernel(tc, x, weight, bias, grid, grad_out, out):
         quantise(6, 0, 2)
         quantise(7, 0, 2)
 
-        order = [(0, t) for t in range(T_TILES)]
-        order += [(n, t) for t in range(T_TILES) for n in (1, 2, 3)]
+        order = [(n, t) for t in range(HEAD_SPLIT) for n in (0, 1)]
+        order += [(0, t) for t in range(HEAD_SPLIT, T_TILES)]
+        order += [(n, t) for t in range(HEAD_SPLIT) for n in (2, 3)]
+        order += [(n, t) for t in range(HEAD_SPLIT, T_TILES) for n in (1, 2, 3)]
         order += [(n, t) for t in range(T_TILES) for n in (4, 5, 6, 7)]
         stage = {}
         stored = {}
@@ -192,7 +195,8 @@ def tile_ant_linear_kernel(tc, x, weight, bias, grid, grad_out, out):
                 nc.scalar.copy(out=dst, in_=acc[:])
             filled[key] = filled[key] + 1
             last_tile = key == (1, T_TILES - 1)
-            if filled[key] == 4 or (last_tile and n in TAIL_STORES_AFTER):
+            head_piece = h == 0 and t < HEAD_SPLIT and n == 1
+            if filled[key] == 4 or head_piece or (last_tile and n in TAIL_STORES_AFTER):
                 lo = NB * stored[key]
                 hi = NB * filled[key]
                 nc.sync.dma_start(

@@ -25,8 +25,7 @@ BYTES = K * COLS * 2 + TOKENS * K * 2 + TOKENS * COLS * 4
 
 MANUAL = True
 LOAD_GROUPS = ((0, 1024), (1024, 1024), (2048, 2048))
-SCALAR_REGROUPS = ((1, 0), (1, 1))
-HEAD_SPLIT = 2
+SCALAR_REGROUPS = ((1, 0), (1, 1), (3, 0), (3, 1))
 VECTOR_EVAC_FROM_BANK = 32
 TAIL_STORES_AFTER = (5, 6, 7)
 RING_BUFS = 5
@@ -36,7 +35,7 @@ def tile_ant_linear_kernel(tc, x, weight, bias, grid, grad_out, out):
     nc = tc.nc
     g_view = grad_out.flatten_outer_dims().rearrange("(p t) k -> p (t k)", t=T_TILES)
     o_view = out.flatten_outer_dims().rearrange("(p t) i -> p t i", t=T_TILES)
-    w_view = weight.rearrange("(c u q e) i -> c u q e i", c=PASSES, u=2, e=2)
+    w_view = weight.rearrange("(c q j) i -> c q j i", c=PASSES, j=4)
 
     with ExitStack() as ctx:
         keep = ctx.enter_context(tc.tile_pool(name="keep", bufs=1))
@@ -61,11 +60,7 @@ def tile_ant_linear_kernel(tc, x, weight, bias, grid, grad_out, out):
                     name="wraw%d_%d" % (c0, c),
                     offset=16 * c0 + 8 * width * c,
                 )
-                for u in range(2):
-                    nc.sync.dma_start(
-                        out=t_w[:, 2 * u : 2 * u + 2, :],
-                        in_=w_view[c, u, :, :, c0 : c0 + width],
-                    )
+                nc.sync.dma_start(out=t_w[:], in_=w_view[c, :, :, c0 : c0 + width])
                 per_pass.append(t_w)
             w_raw.append(per_pass)
 
@@ -75,14 +70,14 @@ def tile_ant_linear_kernel(tc, x, weight, bias, grid, grad_out, out):
         g_codes = []
         g_scales = []
         for hb in range(2):
-            words = g_raw[hb][:].bitcast(F32)
+            words = g_raw[hb][:].bitcast(F32).rearrange("p (s q u) -> p s u q", q=P, u=2)
             g_grp = ring.tile([P, 2048], F32, tag="ring", name="ggrp%d" % hb, align_bytes=64)
             for tl in range(4):
                 xt = psum.tile([P, 512], F32, tag="bank", name="xt")
                 for j in range(4):
                     nc.tensor.transpose(
                         xt[:, P * j : P * (j + 1)],
-                        words[:, 512 * tl + P * j : 512 * tl + P * (j + 1)],
+                        words[:, 2 * tl + j // 2, j % 2, :],
                         ident[:],
                     )
                 dst = g_grp[:, 512 * tl : 512 * (tl + 1)].rearrange(
@@ -142,10 +137,10 @@ def tile_ant_linear_kernel(tc, x, weight, bias, grid, grad_out, out):
         regroup(2, 0)
         regroup(2, 1)
         regroup(3, 0)
-        quantise(2, 0, 2)
         regroup(3, 1)
-        quantise(3, 0, 1)
-        quantise(3, 1, 2)
+        quantise(2, 0, 1)
+        quantise(2, 1, 2)
+        quantise(3, 0, 2)
         for n in range(4, 8):
             alloc(n)
         for n in range(4, 8):
@@ -159,10 +154,8 @@ def tile_ant_linear_kernel(tc, x, weight, bias, grid, grad_out, out):
         quantise(6, 0, 2)
         quantise(7, 0, 2)
 
-        order = [(n, t) for t in range(HEAD_SPLIT) for n in (0, 1)]
-        order += [(0, t) for t in range(HEAD_SPLIT, T_TILES)]
-        order += [(n, t) for t in range(HEAD_SPLIT) for n in (2, 3)]
-        order += [(n, t) for t in range(HEAD_SPLIT, T_TILES) for n in (1, 2, 3)]
+        order = [(0, t) for t in range(T_TILES)]
+        order += [(n, t) for t in range(T_TILES) for n in (1, 2, 3)]
         order += [(n, t) for t in range(T_TILES) for n in (4, 5, 6, 7)]
         stage = {}
         stored = {}
@@ -195,8 +188,7 @@ def tile_ant_linear_kernel(tc, x, weight, bias, grid, grad_out, out):
                 nc.scalar.copy(out=dst, in_=acc[:])
             filled[key] = filled[key] + 1
             last_tile = key == (1, T_TILES - 1)
-            head_piece = h == 0 and t < HEAD_SPLIT and n == 1
-            if filled[key] == 4 or head_piece or (last_tile and n in TAIL_STORES_AFTER):
+            if filled[key] == 4 or (last_tile and n in TAIL_STORES_AFTER):
                 lo = NB * stored[key]
                 hi = NB * filled[key]
                 nc.sync.dma_start(

@@ -27,7 +27,6 @@ MANUAL = True
 LOAD_GROUPS = ((0, 1024), (1024, 1024), (2048, 2048))
 SCALAR_REGROUPS = ((1, 0), (1, 1), (3, 0), (3, 1))
 VECTOR_EVAC_FROM_BANK = 32
-TAIL_STORES_AFTER = (5, 6, 7)
 RING_BUFS = 5
 
 
@@ -35,7 +34,7 @@ def tile_ant_linear_kernel(tc, x, weight, bias, grid, grad_out, out):
     nc = tc.nc
     g_view = grad_out.flatten_outer_dims().rearrange("(p t) k -> p (t k)", t=T_TILES)
     o_view = out.flatten_outer_dims().rearrange("(p t) i -> p t i", t=T_TILES)
-    w_view = weight.rearrange("(c q j) i -> c q j i", c=PASSES, j=4)
+    w_view = weight.rearrange("(c u q e) i -> c u q e i", c=PASSES, u=2, e=2)
 
     with ExitStack() as ctx:
         keep = ctx.enter_context(tc.tile_pool(name="keep", bufs=1))
@@ -60,7 +59,11 @@ def tile_ant_linear_kernel(tc, x, weight, bias, grid, grad_out, out):
                     name="wraw%d_%d" % (c0, c),
                     offset=16 * c0 + 8 * width * c,
                 )
-                nc.sync.dma_start(out=t_w[:], in_=w_view[c, :, :, c0 : c0 + width])
+                for u in range(2):
+                    nc.sync.dma_start(
+                        out=t_w[:, 2 * u : 2 * u + 2, :],
+                        in_=w_view[c, u, :, :, c0 : c0 + width],
+                    )
                 per_pass.append(t_w)
             w_raw.append(per_pass)
 
@@ -70,14 +73,14 @@ def tile_ant_linear_kernel(tc, x, weight, bias, grid, grad_out, out):
         g_codes = []
         g_scales = []
         for hb in range(2):
-            words = g_raw[hb][:].bitcast(F32).rearrange("p (s q u) -> p s u q", q=P, u=2)
+            words = g_raw[hb][:].bitcast(F32)
             g_grp = ring.tile([P, 2048], F32, tag="ring", name="ggrp%d" % hb, align_bytes=64)
             for tl in range(4):
                 xt = psum.tile([P, 512], F32, tag="bank", name="xt")
                 for j in range(4):
                     nc.tensor.transpose(
                         xt[:, P * j : P * (j + 1)],
-                        words[:, 2 * tl + j // 2, j % 2, :],
+                        words[:, 512 * tl + P * j : 512 * tl + P * (j + 1)],
                         ident[:],
                     )
                 dst = g_grp[:, 512 * tl : 512 * (tl + 1)].rearrange(
@@ -158,7 +161,6 @@ def tile_ant_linear_kernel(tc, x, weight, bias, grid, grad_out, out):
         order += [(n, t) for t in range(T_TILES) for n in (1, 2, 3)]
         order += [(n, t) for t in range(T_TILES) for n in (4, 5, 6, 7)]
         stage = {}
-        stored = {}
         filled = {}
         for bank, (n, t) in enumerate(order):
             h = n // 4
@@ -167,7 +169,6 @@ def tile_ant_linear_kernel(tc, x, weight, bias, grid, grad_out, out):
                 stage[key] = flat.tile(
                     [P, HALF], F32, name="stage%d_%d" % key, offset=65536 * (1 - h) + 8192 * t
                 )
-                stored[key] = 0
                 filled[key] = 0
             acc = psum.tile([P, NB], F32, tag="bank", name="acc")
             for c in range(PASSES):
@@ -187,11 +188,7 @@ def tile_ant_linear_kernel(tc, x, weight, bias, grid, grad_out, out):
             else:
                 nc.scalar.copy(out=dst, in_=acc[:])
             filled[key] = filled[key] + 1
-            last_tile = key == (1, T_TILES - 1)
-            if filled[key] == 4 or (last_tile and n in TAIL_STORES_AFTER):
-                lo = NB * stored[key]
-                hi = NB * filled[key]
+            if filled[key] == 4:
                 nc.sync.dma_start(
-                    out=o_view[:, t, HALF * h + lo : HALF * h + hi], in_=stage[key][:, lo:hi]
+                    out=o_view[:, t, HALF * h : HALF * (h + 1)], in_=stage[key][:]
                 )
-                stored[key] = filled[key]

from contextlib import ExitStack

import concourse.mybir as mybir
from concourse.masks import make_identity

F32 = mybir.dt.float32
BF16 = mybir.dt.bfloat16
U32 = mybir.dt.uint32
U8 = mybir.dt.uint8
E4X4 = mybir.dt.float8_e4m3fn_x4
E5X4 = mybir.dt.float8_e5m2_x4

P = 128
TOKENS = 1024
K = 1024
COLS = 4096
T_TILES = TOKENS // P
PASSES = K // 512
NB = 512
BLOCKS = COLS // NB
HALF = COLS // 2

FLOPS = 2 * TOKENS * K * COLS
BYTES = K * COLS * 2 + TOKENS * K * 2 + TOKENS * COLS * 4

MANUAL = True
LOAD_GROUPS = ((0, 1024), (1024, 1024), (2048, 2048))
SCALAR_REGROUPS = ((1, 0), (1, 1), (3, 0), (3, 1))
VECTOR_EVAC_FROM_BANK = 32
RING_BUFS = 5


def tile_ant_linear_kernel(tc, x, weight, bias, grid, grad_out, out):
    nc = tc.nc
    g_view = grad_out.flatten_outer_dims().rearrange("(p t) k -> p (t k)", t=T_TILES)
    o_view = out.flatten_outer_dims().rearrange("(p t) i -> p t i", t=T_TILES)
    w_view = weight.rearrange("(c u q e) i -> c u q e i", c=PASSES, u=2, e=2)

    with ExitStack() as ctx:
        keep = ctx.enter_context(tc.tile_pool(name="keep", bufs=1))
        flat = ctx.enter_context(tc.tile_pool(name="flat", bufs=1))
        ring = ctx.enter_context(tc.tile_pool(name="ring", bufs=RING_BUFS))
        psum = ctx.enter_context(tc.psum_pool(name="psum", bufs=8))
        if MANUAL:
            ctx.enter_context(tc.manual_schedule())

        g_raw = []
        for hb in range(2):
            t_raw = ring.tile([P, 4096], BF16, tag="ring", name="graw%d" % hb, align_bytes=64)
            nc.sync.dma_start(out=t_raw[:], in_=g_view[:, 4096 * hb : 4096 * (hb + 1)])
            g_raw.append(t_raw)
        w_raw = []
        for c0, width in LOAD_GROUPS:
            per_pass = []
            for c in range(PASSES):
                t_w = flat.tile(
                    [P, 4, width],
                    BF16,
                    name="wraw%d_%d" % (c0, c),
                    offset=16 * c0 + 8 * width * c,
                )
                for u in range(2):
                    nc.sync.dma_start(
                        out=t_w[:, 2 * u : 2 * u + 2, :],
                        in_=w_view[c, u, :, :, c0 : c0 + width],
                    )
                per_pass.append(t_w)
            w_raw.append(per_pass)

        ident = keep.tile([P, P], F32, name="ident")
        make_identity(nc, ident[:])

        g_codes = []
        g_scales = []
        for hb in range(2):
            words = g_raw[hb][:].bitcast(F32)
            g_grp = ring.tile([P, 2048], F32, tag="ring", name="ggrp%d" % hb, align_bytes=64)
            for tl in range(4):
                xt = psum.tile([P, 512], F32, tag="bank", name="xt")
                for j in range(4):
                    nc.tensor.transpose(
                        xt[:, P * j : P * (j + 1)],
                        words[:, 512 * tl + P * j : 512 * tl + P * (j + 1)],
                        ident[:],
                    )
                dst = g_grp[:, 512 * tl : 512 * (tl + 1)].rearrange(
                    "p (c r u) -> p c r u", c=2, u=2
                )
                src = xt[:].rearrange("p (c u r) -> p c r u", c=2, u=2)
                if tl % 2 == 0:
                    nc.scalar.copy(out=dst, in_=src)
                else:
                    nc.vector.tensor_copy(out=dst, in_=src)
            codes = keep.tile([P, 1024], U32, name="gcodes%d" % hb, align_bytes=64)
            scales = keep.tile([P, 1024], U8, name="gscales%d" % hb, align_bytes=64)
            nc.vector.quantize_mx(
                out=codes[:].bitcast(E5X4), scales=scales[:], in_=g_grp[:].bitcast(BF16)
            )
            g_codes.append(codes)
            g_scales.append(scales)

        w_grp = {}
        w_codes = {}
        w_scales = {}

        def alloc(n):
            w_grp[n] = ring.tile([P, 4096], BF16, tag="ring", name="wgrp%d" % n, align_bytes=64)
            w_codes[n] = keep.tile([P, 1024], U32, name="wcodes%d" % n, align_bytes=64)
            w_scales[n] = keep.tile([P, 1024], U8, name="wscales%d" % n, align_bytes=64)

        def regroup(n, c):
            col = n * NB
            gi = [i for i, (c0, width) in enumerate(LOAD_GROUPS) if c0 <= col < c0 + width][0]
            off = col - LOAD_GROUPS[gi][0]
            src = w_raw[gi][c][:, :, off : off + NB].rearrange("p t (a i) -> p a t i", i=4)
            dst = w_grp[n][:, 2048 * c : 2048 * (c + 1)].rearrange(
                "p (a i t) -> p a t i", i=4, t=4
            )
            if (n, c) in SCALAR_REGROUPS:
                nc.scalar.copy(out=dst, in_=src)
            else:
                nc.vector.tensor_copy(out=dst, in_=src)

        def quantise(n, lo, hi):
            nc.vector.quantize_mx(
                out=w_codes[n][:, 512 * lo : 512 * hi].bitcast(E4X4),
                scales=w_scales[n][:, 512 * lo : 512 * hi],
                in_=w_grp[n][:, 2048 * lo : 2048 * hi],
            )

        for n in range(4):
            alloc(n)
        regroup(0, 0)
        regroup(0, 1)
        regroup(1, 0)
        regroup(1, 1)
        quantise(0, 0, 1)
        quantise(0, 1, 2)
        quantise(1, 0, 2)
        regroup(2, 0)
        regroup(2, 1)
        regroup(3, 0)
        regroup(3, 1)
        quantise(2, 0, 1)
        quantise(2, 1, 2)
        quantise(3, 0, 2)
        for n in range(4, 8):
            alloc(n)
        for n in range(4, 8):
            regroup(n, 0)
        regroup(4, 1)
        regroup(5, 1)
        quantise(4, 0, 2)
        regroup(6, 1)
        quantise(5, 0, 2)
        regroup(7, 1)
        quantise(6, 0, 2)
        quantise(7, 0, 2)

        order = [(0, t) for t in range(T_TILES)]
        order += [(n, t) for t in range(T_TILES) for n in (1, 2, 3)]
        order += [(n, t) for t in range(T_TILES) for n in (4, 5, 6, 7)]
        stage = {}
        filled = {}
        for bank, (n, t) in enumerate(order):
            h = n // 4
            key = (h, t)
            if key not in stage:
                stage[key] = flat.tile(
                    [P, HALF], F32, name="stage%d_%d" % key, offset=65536 * (1 - h) + 8192 * t
                )
                filled[key] = 0
            acc = psum.tile([P, NB], F32, tag="bank", name="acc")
            for c in range(PASSES):
                sl = slice(P * (2 * (t % 4) + c), P * (2 * (t % 4) + c + 1))
                nc.tensor.matmul_mx(
                    out=acc[:],
                    lhsT=g_codes[t // 4][:, sl].bitcast(E5X4),
                    lhsT_scale=g_scales[t // 4][:, sl],
                    rhs=w_codes[n][:, 512 * c : 512 * (c + 1)].bitcast(E4X4),
                    rhs_scale=w_scales[n][:, 512 * c : 512 * (c + 1)],
                    start=(c == 0),
                    stop=(c == PASSES - 1),
                )
            dst = stage[key][:, NB * (n % 4) : NB * (n % 4 + 1)]
            if bank >= VECTOR_EVAC_FROM_BANK and bank % 2 == 1:
                nc.vector.tensor_copy(out=dst, in_=acc[:])
            else:
                nc.scalar.copy(out=dst, in_=acc[:])
            filled[key] = filled[key] + 1
            if filled[key] == 4:
                nc.sync.dma_start(
                    out=o_view[:, t, HALF * h : HALF * (h + 1)], in_=stage[key][:]
                )
